import numpy as np
import ml_dtypes

BF16 = ml_dtypes.bfloat16


def bf(x):
    return np.asarray(x, np.float32).astype(BF16)


def f32(x):
    return np.asarray(x, np.float32)


def f64(x):
    return np.asarray(x).astype(np.float64)


def striped(idx):
    return np.tile(idx.reshape(-1, 16).T, (8, 1))


V, D, T, B, U, TU, N = 4096, 128, 16, 128, 128, 128, 2048


def softmax(z, axis):
    e = np.exp(z - z.max(axis=axis, keepdims=True))
    return e / e.sum(axis=axis, keepdims=True)


def setup_inputs():
    return {"table": bf(np.random.standard_normal((D, V))), "w": bf(np.random.standard_normal((D, D)) / np.sqrt(D)), "a": bf(np.random.standard_normal((D, 1))), "clicked": bf(np.random.standard_normal((TU, U))), "w_u": bf(0.4 * np.random.standard_normal((TU, D)) / np.sqrt(TU)), "b_u": f32(0.1 * np.random.standard_normal((D, 1))), "offs": striped(np.random.permutation(np.tile(np.arange(V), 2))[:N])}


def reference(table, w, a, clicked, w_u, b_u, offs):
    idx = offs[:16].T.reshape(-1)
    e = f64(table)[:, idx]
    v = (f64(w).T @ e).reshape(D, B, T)
    s = (f64(a)[:, 0] @ e).reshape(B, T) / np.sqrt(D)
    news = (softmax(s, -1)[None] * v).sum(axis=-1)
    user = f64(w_u).T @ f64(clicked) + f64(b_u)
    return softmax(user.T @ news, -1)

@@ -1,0 +1,106 @@
+import math
+
+import concourse.mybir as mybir
+
+BF16, F32, U16 = mybir.dt.bfloat16, mybir.dt.float32, mybir.dt.uint16
+ALU = mybir.AluOpType
+EXP = mybir.ActivationFunctionType.Exp
+X = mybir.AxisListType.X
+
+P = 128
+V = 4096
+N = 2048
+WORDS = 16
+TITLES = N // WORDS
+PIECE = 512
+PIECES = N // PIECE
+PIECE_TITLES = PIECE // WORDS
+
+FLOPS = 2 * P * P * N + 2 * P * N + 2 * P * N + 2 * P * P * P + 2 * P * P * TITLES
+
+
+def tile_nrmsmodel_kernel(tc, table, w, a, clicked, w_u, b_u, offs, out):
+    nc = tc.nc
+    with (
+        tc.tile_pool(name="held", bufs=1) as held,
+        tc.tile_pool(name="work", bufs=2) as work,
+        tc.psum_pool(name="psum", bufs=2) as psum,
+    ):
+        offsets = held.tile([P, N // 16], U16, name="offsets")
+        nc.sync.dma_start(offsets[:], offs)
+        table_sb = held.tile([P, V], BF16, name="table_sb")
+        nc.sync.dma_start(table_sb[:], table)
+
+        a_row = held.tile([1, P], BF16, name="a_row")
+        nc.scalar.dma_start(a_row[:], a.rearrange("k o -> o k"))
+        w_sb = held.tile([P, P], BF16, name="w_sb")
+        nc.scalar.dma_start(w_sb[:], w)
+        w_u_sb = held.tile([P, P], BF16, name="w_u_sb")
+        nc.scalar.dma_start(w_u_sb[:], w_u)
+        clicked_sb = held.tile([P, P], BF16, name="clicked_sb")
+        nc.scalar.dma_start(clicked_sb[:], clicked)
+        b_row = held.tile([1, P], F32, name="b_row")
+        nc.scalar.dma_start(b_row[:], b_u.rearrange("m o -> o m"))
+
+        ones_bf = held.tile([1, P], BF16, name="ones_bf")
+        nc.vector.memset(ones_bf[:], 1.0)
+        ones_f = held.tile([1, P], F32, name="ones_f")
+        nc.vector.memset(ones_f[:], 1.0)
+
+        a_ps = psum.tile([P, P], F32, name="a_ps", tag="small")
+        nc.tensor.matmul(a_ps[:], a_row[:], ones_bf[:], start=True, stop=True)
+        a_all = held.tile([P, P], BF16, name="a_all")
+        nc.vector.tensor_copy(a_all[:], a_ps[:])
+
+        user_ps = psum.tile([P, P], F32, name="user_ps", tag="small")
+        nc.tensor.matmul(user_ps[:], w_u_sb[:], clicked_sb[:], start=True, stop=False)
+        nc.tensor.matmul(user_ps[:], b_row[:], ones_f[:], start=False, stop=True)
+        user_bf = held.tile([P, P], BF16, name="user_bf")
+        nc.vector.tensor_copy(user_bf[:], user_ps[:])
+
+        top = held.tile([P, TITLES], F32, name="top")
+        num = held.tile([P, TITLES], F32, name="num")
+        den = held.tile([P, TITLES], F32, name="den")
+        for c in range(PIECES):
+            looked_up = table_sb[:].indirect(offsets[:, c * (PIECE // 16) : (c + 1) * (PIECE // 16)])
+            titles = slice(c * PIECE_TITLES, (c + 1) * PIECE_TITLES)
+            by_title = [P, PIECE_TITLES, WORDS]
+
+            s_ps = psum.tile([P, PIECE], F32, name="s_ps")
+            nc.tensor.matmul(s_ps[:], a_all[:], looked_up, start=True, stop=True)
+            v_ps = psum.tile([P, PIECE], F32, name="v_ps")
+            nc.tensor.matmul(v_ps[:], w_sb[:], looked_up, start=True, stop=True)
+
+            s_3d = s_ps[:].rearrange("p (n t) -> p n t", t=WORDS)
+            nc.vector.reduce_max(top[:, titles], s_3d, axis=X)
+            shifted = work.tile([P, PIECE], F32, name="shifted")
+            nc.vector.tensor_tensor(
+                shifted[:].rearrange("p (n t) -> p n t", t=WORDS),
+                s_3d,
+                top[:, titles].unsqueeze(2).to_broadcast(by_title),
+                ALU.subtract,
+            )
+            e = work.tile([P, PIECE], F32, name="e")
+            nc.scalar.activation(e[:], shifted[:], EXP, scale=1.0 / math.sqrt(P))
+            ev = work.tile([P, PIECE], F32, name="ev")
+            nc.vector.tensor_tensor(ev[:], v_ps[:], e[:], ALU.mult)
+            nc.vector.reduce_sum(num[:, titles], ev[:].rearrange("p (n t) -> p n t", t=WORDS), axis=X)
+            nc.vector.reduce_sum(den[:, titles], e[:].rearrange("p (n t) -> p n t", t=WORDS), axis=X)
+
+        rden = held.tile([P, TITLES], F32, name="rden")
+        nc.vector.reciprocal(rden[:], den[:])
+        news_bf = held.tile([P, TITLES], BF16, name="news_bf")
+        nc.vector.tensor_tensor(news_bf[:], num[:], rden[:], ALU.mult)
+
+        logit_ps = psum.tile([P, TITLES], F32, name="logit_ps", tag="small")
+        nc.tensor.matmul(logit_ps[:], user_bf[:], news_bf[:], start=True, stop=True)
+        neg_max = held.tile([P, 1], F32, name="neg_max")
+        nc.vector.reduce_max(neg_max[:], logit_ps[:], axis=X, negate=True)
+        el = held.tile([P, TITLES], F32, name="el")
+        el_sum = held.tile([P, 1], F32, name="el_sum")
+        nc.scalar.activation(el[:], logit_ps[:], EXP, bias=neg_max[:], accum_out=el_sum[:])
+        r_sum = held.tile([P, 1], F32, name="r_sum")
+        nc.vector.reciprocal(r_sum[:], el_sum[:])
+        out_sb = held.tile([P, TITLES], F32, name="out_sb")
+        nc.vector.tensor_scalar_mul(out_sb[:], el[:], r_sum[:])
+        nc.sync.dma_start(out, out_sb[:])

@@ -15,16 +15,21 @@ TITLES = N // WORDS
 PIECE = 512
 PIECES = N // PIECE
 PIECE_TITLES = PIECE // WORDS
+BANKS = 8
+FOLDS = 2
 
 FLOPS = 2 * P * P * N + 2 * P * N + 2 * P * N + 2 * P * P * P + 2 * P * P * TITLES
+
+
+def words(ap):
+    return ap.rearrange("p (n t) -> p n t", t=WORDS)
 
 
 def tile_nrmsmodel_kernel(tc, table, w, a, clicked, w_u, b_u, offs, out):
     nc = tc.nc
     with (
         tc.tile_pool(name="held", bufs=1) as held,
-        tc.tile_pool(name="work", bufs=2) as work,
-        tc.psum_pool(name="psum", bufs=2) as psum,
+        tc.psum_pool(name="psum", bufs=BANKS) as psum,
     ):
         offsets = held.tile([P, N // 16], U16, name="offsets")
         nc.sync.dma_start(offsets[:], offs)
@@ -47,52 +52,68 @@ def tile_nrmsmodel_kernel(tc, table, w, a, clicked, w_u, b_u, offs, out):
         ones_f = held.tile([1, P], F32, name="ones_f")
         nc.vector.memset(ones_f[:], 1.0)
 
-        a_ps = psum.tile([P, P], F32, name="a_ps", tag="small")
+        a_ps = psum.tile([P, P], F32, name="a_ps", tag="bank")
         nc.tensor.matmul(a_ps[:], a_row[:], ones_bf[:], start=True, stop=True)
         a_all = held.tile([P, P], BF16, name="a_all")
         nc.vector.tensor_copy(a_all[:], a_ps[:])
 
-        user_ps = psum.tile([P, P], F32, name="user_ps", tag="small")
+        user_ps = psum.tile([P, P], F32, name="user_ps", tag="bank")
         nc.tensor.matmul(user_ps[:], w_u_sb[:], clicked_sb[:], start=True, stop=False)
         nc.tensor.matmul(user_ps[:], b_row[:], ones_f[:], start=False, stop=True)
         user_bf = held.tile([P, P], BF16, name="user_bf")
         nc.vector.tensor_copy(user_bf[:], user_ps[:])
 
-        top = held.tile([P, TITLES], F32, name="top")
-        num = held.tile([P, TITLES], F32, name="num")
-        den = held.tile([P, TITLES], F32, name="den")
+        pieces = [slice(c * PIECE, (c + 1) * PIECE) for c in range(PIECES)]
+        titles = [slice(c * PIECE_TITLES, (c + 1) * PIECE_TITLES) for c in range(PIECES)]
+        looked_up = [
+            table_sb[:].indirect(offsets[:, c * (PIECE // 16) : (c + 1) * (PIECE // 16)]) for c in range(PIECES)
+        ]
+        s_ps = [psum.tile([P, PIECE], F32, name="s_ps" + str(c), tag="bank") for c in range(PIECES)]
+        v_ps = [psum.tile([P, PIECE], F32, name="v_ps" + str(c), tag="bank") for c in range(PIECES)]
         for c in range(PIECES):
-            looked_up = table_sb[:].indirect(offsets[:, c * (PIECE // 16) : (c + 1) * (PIECE // 16)])
-            titles = slice(c * PIECE_TITLES, (c + 1) * PIECE_TITLES)
-            by_title = [P, PIECE_TITLES, WORDS]
+            nc.tensor.matmul(s_ps[c][:], a_all[:], looked_up[c], start=True, stop=True)
+        for c in range(PIECES):
+            nc.tensor.matmul(v_ps[c][:], w_sb[:], looked_up[c], start=True, stop=True)
 
-            s_ps = psum.tile([P, PIECE], F32, name="s_ps")
-            nc.tensor.matmul(s_ps[:], a_all[:], looked_up, start=True, stop=True)
-            v_ps = psum.tile([P, PIECE], F32, name="v_ps")
-            nc.tensor.matmul(v_ps[:], w_sb[:], looked_up, start=True, stop=True)
-
-            s_3d = s_ps[:].rearrange("p (n t) -> p n t", t=WORDS)
-            nc.vector.reduce_max(top[:, titles], s_3d, axis=X)
-            shifted = work.tile([P, PIECE], F32, name="shifted")
+        top = held.tile([P, TITLES], F32, name="top")
+        shifted = held.tile([P, N], F32, name="shifted")
+        e = held.tile([P, N], F32, name="e")
+        for c in range(PIECES):
+            nc.vector.reduce_max(top[:, titles[c]], words(s_ps[c][:]), axis=X)
             nc.vector.tensor_tensor(
-                shifted[:].rearrange("p (n t) -> p n t", t=WORDS),
-                s_3d,
-                top[:, titles].unsqueeze(2).to_broadcast(by_title),
+                words(shifted[:, pieces[c]]),
+                words(s_ps[c][:]),
+                top[:, titles[c]].unsqueeze(2).to_broadcast([P, PIECE_TITLES, WORDS]),
                 ALU.subtract,
             )
-            e = work.tile([P, PIECE], F32, name="e")
-            nc.scalar.activation(e[:], shifted[:], EXP, scale=1.0 / math.sqrt(P))
-            ev = work.tile([P, PIECE], F32, name="ev")
-            nc.vector.tensor_tensor(ev[:], v_ps[:], e[:], ALU.mult)
-            nc.vector.reduce_sum(num[:, titles], ev[:].rearrange("p (n t) -> p n t", t=WORDS), axis=X)
-            nc.vector.reduce_sum(den[:, titles], e[:].rearrange("p (n t) -> p n t", t=WORDS), axis=X)
+            nc.scalar.activation(e[:, pieces[c]], shifted[:, pieces[c]], EXP, scale=1.0 / math.sqrt(P))
+
+        den = held.tile([P, TITLES], F32, name="den")
+        for h in range(FOLDS):
+            folded = words(e[:, h * (N // FOLDS) : (h + 1) * (N // FOLDS)])
+            for half in (8, 4, 2):
+                shorter = held.tile([P, TITLES // FOLDS, half], F32, name="fold" + str(h) + "_" + str(half))
+                nc.gpsimd.tensor_tensor(shorter[:], folded[:, :, 0:half], folded[:, :, half : 2 * half], ALU.add)
+                folded = shorter[:]
+            nc.gpsimd.tensor_tensor(
+                den[:, h * (TITLES // FOLDS) : (h + 1) * (TITLES // FOLDS)].unsqueeze(2),
+                folded[:, :, 0:1],
+                folded[:, :, 1:2],
+                ALU.add,
+            )
+
+        ev = held.tile([P, N], F32, name="ev")
+        num = held.tile([P, TITLES], F32, name="num")
+        for c in range(PIECES):
+            nc.vector.tensor_tensor(ev[:, pieces[c]], v_ps[c][:], e[:, pieces[c]], ALU.mult)
+            nc.vector.reduce_sum(num[:, titles[c]], words(ev[:, pieces[c]]), axis=X)
 
         rden = held.tile([P, TITLES], F32, name="rden")
         nc.vector.reciprocal(rden[:], den[:])
         news_bf = held.tile([P, TITLES], BF16, name="news_bf")
         nc.vector.tensor_tensor(news_bf[:], num[:], rden[:], ALU.mult)
 
-        logit_ps = psum.tile([P, TITLES], F32, name="logit_ps", tag="small")
+        logit_ps = psum.tile([P, TITLES], F32, name="logit_ps", tag="bank")
         nc.tensor.matmul(logit_ps[:], user_bf[:], news_bf[:], start=True, stop=True)
         neg_max = held.tile([P, 1], F32, name="neg_max")
         nc.vector.reduce_max(neg_max[:], logit_ps[:], axis=X, negate=True)

@@ -16,7 +16,6 @@ PIECE = 512
 PIECES = N // PIECE
 PIECE_TITLES = PIECE // WORDS
 BANKS = 8
-FOLDS = 2
 
 FLOPS = 2 * P * P * N + 2 * P * N + 2 * P * N + 2 * P * P * P + 2 * P * P * TITLES
 
@@ -89,14 +88,14 @@ def tile_nrmsmodel_kernel(tc, table, w, a, clicked, w_u, b_u, offs, out):
             nc.scalar.activation(e[:, pieces[c]], shifted[:, pieces[c]], EXP, scale=1.0 / math.sqrt(P))
 
         den = held.tile([P, TITLES], F32, name="den")
-        for h in range(FOLDS):
-            folded = words(e[:, h * (N // FOLDS) : (h + 1) * (N // FOLDS)])
+        for first, count in ((0, 1), (1, 1), (2, 2)):
+            folded = words(e[:, first * PIECE : (first + count) * PIECE])
             for half in (8, 4, 2):
-                shorter = held.tile([P, TITLES // FOLDS, half], F32, name="fold" + str(h) + "_" + str(half))
+                shorter = held.tile([P, count * PIECE_TITLES, half], F32, name="fold" + str(first) + "_" + str(half))
                 nc.gpsimd.tensor_tensor(shorter[:], folded[:, :, 0:half], folded[:, :, half : 2 * half], ALU.add)
                 folded = shorter[:]
             nc.gpsimd.tensor_tensor(
-                den[:, h * (TITLES // FOLDS) : (h + 1) * (TITLES // FOLDS)].unsqueeze(2),
+                den[:, first * PIECE_TITLES : (first + count) * PIECE_TITLES].unsqueeze(2),
                 folded[:, :, 0:1],
                 folded[:, :, 1:2],
                 ALU.add,

@@ -16,6 +16,8 @@ PIECE = 512
 PIECES = N // PIECE
 PIECE_TITLES = PIECE // WORDS
 BANKS = 8
+WARM_UPS = 8
+FOLDS = 2
 
 FLOPS = 2 * P * P * N + 2 * P * N + 2 * P * N + 2 * P * P * P + 2 * P * P * TITLES
 
@@ -50,6 +52,12 @@ def tile_nrmsmodel_kernel(tc, table, w, a, clicked, w_u, b_u, offs, out):
         nc.vector.memset(ones_bf[:], 1.0)
         ones_f = held.tile([1, P], F32, name="ones_f")
         nc.vector.memset(ones_f[:], 1.0)
+
+        zeros = held.tile([P, PIECE], BF16, name="zeros")
+        nc.vector.memset(zeros[:], 0.0)
+        warm_ps = psum.tile([P, PIECE], F32, name="warm_ps", tag="bank")
+        for i in range(WARM_UPS):
+            nc.tensor.matmul(warm_ps[:], zeros[:, 0:P], zeros[:], start=True, stop=True)
 
         a_ps = psum.tile([P, P], F32, name="a_ps", tag="bank")
         nc.tensor.matmul(a_ps[:], a_row[:], ones_bf[:], start=True, stop=True)
@@ -88,14 +96,14 @@ def tile_nrmsmodel_kernel(tc, table, w, a, clicked, w_u, b_u, offs, out):
             nc.scalar.activation(e[:, pieces[c]], shifted[:, pieces[c]], EXP, scale=1.0 / math.sqrt(P))
 
         den = held.tile([P, TITLES], F32, name="den")
-        for first, count in ((0, 1), (1, 1), (2, 2)):
-            folded = words(e[:, first * PIECE : (first + count) * PIECE])
+        for h in range(FOLDS):
+            folded = words(e[:, h * (N // FOLDS) : (h + 1) * (N // FOLDS)])
             for half in (8, 4, 2):
-                shorter = held.tile([P, count * PIECE_TITLES, half], F32, name="fold" + str(first) + "_" + str(half))
+                shorter = held.tile([P, TITLES // FOLDS, half], F32, name="fold" + str(h) + "_" + str(half))
                 nc.gpsimd.tensor_tensor(shorter[:], folded[:, :, 0:half], folded[:, :, half : 2 * half], ALU.add)
                 folded = shorter[:]
             nc.gpsimd.tensor_tensor(
-                den[:, first * PIECE_TITLES : (first + count) * PIECE_TITLES].unsqueeze(2),
+                den[:, h * (TITLES // FOLDS) : (h + 1) * (TITLES // FOLDS)].unsqueeze(2),
                 folded[:, :, 0:1],
                 folded[:, :, 1:2],
                 ALU.add,

@@ -16,7 +16,6 @@ PIECE = 512
 PIECES = N // PIECE
 PIECE_TITLES = PIECE // WORDS
 BANKS = 8
-WARM_UPS = 8
 FOLDS = 2
 
 FLOPS = 2 * P * P * N + 2 * P * N + 2 * P * N + 2 * P * P * P + 2 * P * P * TITLES
@@ -34,41 +33,28 @@ def tile_nrmsmodel_kernel(tc, table, w, a, clicked, w_u, b_u, offs, out):
     ):
         offsets = held.tile([P, N // 16], U16, name="offsets")
         nc.sync.dma_start(offsets[:], offs)
-        table_sb = held.tile([P, V], BF16, name="table_sb")
-        nc.sync.dma_start(table_sb[:], table)
-
         a_row = held.tile([1, P], BF16, name="a_row")
         nc.scalar.dma_start(a_row[:], a.rearrange("k o -> o k"))
+        table_sb = held.tile([P, V], BF16, name="table_sb")
+        nc.sync.dma_start(table_sb[:], table)
         w_sb = held.tile([P, P], BF16, name="w_sb")
-        nc.scalar.dma_start(w_sb[:], w)
+        nc.sync.dma_start(w_sb[:], w)
         w_u_sb = held.tile([P, P], BF16, name="w_u_sb")
-        nc.scalar.dma_start(w_u_sb[:], w_u)
+        nc.sync.dma_start(w_u_sb[:], w_u)
         clicked_sb = held.tile([P, P], BF16, name="clicked_sb")
-        nc.scalar.dma_start(clicked_sb[:], clicked)
+        nc.sync.dma_start(clicked_sb[:], clicked)
         b_row = held.tile([1, P], F32, name="b_row")
-        nc.scalar.dma_start(b_row[:], b_u.rearrange("m o -> o m"))
+        nc.sync.dma_start(b_row[:], b_u.rearrange("m o -> o m"))
 
         ones_bf = held.tile([1, P], BF16, name="ones_bf")
         nc.vector.memset(ones_bf[:], 1.0)
         ones_f = held.tile([1, P], F32, name="ones_f")
         nc.vector.memset(ones_f[:], 1.0)
 
-        zeros = held.tile([P, PIECE], BF16, name="zeros")
-        nc.vector.memset(zeros[:], 0.0)
-        warm_ps = psum.tile([P, PIECE], F32, name="warm_ps", tag="bank")
-        for i in range(WARM_UPS):
-            nc.tensor.matmul(warm_ps[:], zeros[:, 0:P], zeros[:], start=True, stop=True)
-
         a_ps = psum.tile([P, P], F32, name="a_ps", tag="bank")
         nc.tensor.matmul(a_ps[:], a_row[:], ones_bf[:], start=True, stop=True)
         a_all = held.tile([P, P], BF16, name="a_all")
         nc.vector.tensor_copy(a_all[:], a_ps[:])
-
-        user_ps = psum.tile([P, P], F32, name="user_ps", tag="bank")
-        nc.tensor.matmul(user_ps[:], w_u_sb[:], clicked_sb[:], start=True, stop=False)
-        nc.tensor.matmul(user_ps[:], b_row[:], ones_f[:], start=False, stop=True)
-        user_bf = held.tile([P, P], BF16, name="user_bf")
-        nc.vector.tensor_copy(user_bf[:], user_ps[:])
 
         pieces = [slice(c * PIECE, (c + 1) * PIECE) for c in range(PIECES)]
         titles = [slice(c * PIECE_TITLES, (c + 1) * PIECE_TITLES) for c in range(PIECES)]
@@ -81,6 +67,12 @@ def tile_nrmsmodel_kernel(tc, table, w, a, clicked, w_u, b_u, offs, out):
             nc.tensor.matmul(s_ps[c][:], a_all[:], looked_up[c], start=True, stop=True)
         for c in range(PIECES):
             nc.tensor.matmul(v_ps[c][:], w_sb[:], looked_up[c], start=True, stop=True)
+
+        user_ps = psum.tile([P, P], F32, name="user_ps", tag="bank")
+        nc.tensor.matmul(user_ps[:], w_u_sb[:], clicked_sb[:], start=True, stop=False)
+        nc.tensor.matmul(user_ps[:], b_row[:], ones_f[:], start=False, stop=True)
+        user_bf = held.tile([P, P], BF16, name="user_bf")
+        nc.vector.tensor_copy(user_bf[:], user_ps[:])
 
         top = held.tile([P, TITLES], F32, name="top")
         shifted = held.tile([P, N], F32, name="shifted")

@@ -68,12 +68,6 @@ def tile_nrmsmodel_kernel(tc, table, w, a, clicked, w_u, b_u, offs, out):
         for c in range(PIECES):
             nc.tensor.matmul(v_ps[c][:], w_sb[:], looked_up[c], start=True, stop=True)
 
-        user_ps = psum.tile([P, P], F32, name="user_ps", tag="bank")
-        nc.tensor.matmul(user_ps[:], w_u_sb[:], clicked_sb[:], start=True, stop=False)
-        nc.tensor.matmul(user_ps[:], b_row[:], ones_f[:], start=False, stop=True)
-        user_bf = held.tile([P, P], BF16, name="user_bf")
-        nc.vector.tensor_copy(user_bf[:], user_ps[:])
-
         top = held.tile([P, TITLES], F32, name="top")
         shifted = held.tile([P, N], F32, name="shifted")
         e = held.tile([P, N], F32, name="e")
@@ -111,6 +105,12 @@ def tile_nrmsmodel_kernel(tc, table, w, a, clicked, w_u, b_u, offs, out):
         nc.vector.reciprocal(rden[:], den[:])
         news_bf = held.tile([P, TITLES], BF16, name="news_bf")
         nc.vector.tensor_tensor(news_bf[:], num[:], rden[:], ALU.mult)
+
+        user_ps = psum.tile([P, P], F32, name="user_ps", tag="bank")
+        nc.tensor.matmul(user_ps[:], w_u_sb[:], clicked_sb[:], start=True, stop=False)
+        nc.tensor.matmul(user_ps[:], b_row[:], ones_f[:], start=False, stop=True)
+        user_bf = held.tile([P, P], BF16, name="user_bf")
+        nc.vector.tensor_copy(user_bf[:], user_ps[:])
 
         logit_ps = psum.tile([P, TITLES], F32, name="logit_ps", tag="bank")
         nc.tensor.matmul(logit_ps[:], user_bf[:], news_bf[:], start=True, stop=True)

@@ -16,7 +16,7 @@ PIECE = 512
 PIECES = N // PIECE
 PIECE_TITLES = PIECE // WORDS
 BANKS = 8
-FOLDS = 2
+TABLE_LOADS = 2
 
 FLOPS = 2 * P * P * N + 2 * P * N + 2 * P * N + 2 * P * P * P + 2 * P * P * TITLES
 
@@ -36,7 +36,9 @@ def tile_nrmsmodel_kernel(tc, table, w, a, clicked, w_u, b_u, offs, out):
         a_row = held.tile([1, P], BF16, name="a_row")
         nc.scalar.dma_start(a_row[:], a.rearrange("k o -> o k"))
         table_sb = held.tile([P, V], BF16, name="table_sb")
-        nc.sync.dma_start(table_sb[:], table)
+        for i in range(TABLE_LOADS):
+            columns = slice(i * (V // TABLE_LOADS), (i + 1) * (V // TABLE_LOADS))
+            nc.sync.dma_start(table_sb[:, columns], table[:, columns])
         w_sb = held.tile([P, P], BF16, name="w_sb")
         nc.sync.dma_start(w_sb[:], w)
         w_u_sb = held.tile([P, P], BF16, name="w_u_sb")
@@ -82,18 +84,14 @@ def tile_nrmsmodel_kernel(tc, table, w, a, clicked, w_u, b_u, offs, out):
             nc.scalar.activation(e[:, pieces[c]], shifted[:, pieces[c]], EXP, scale=1.0 / math.sqrt(P))
 
         den = held.tile([P, TITLES], F32, name="den")
-        for h in range(FOLDS):
-            folded = words(e[:, h * (N // FOLDS) : (h + 1) * (N // FOLDS)])
+        for c in range(PIECES - 1):
+            folded = words(e[:, pieces[c]])
             for half in (8, 4, 2):
-                shorter = held.tile([P, TITLES // FOLDS, half], F32, name="fold" + str(h) + "_" + str(half))
+                shorter = held.tile([P, PIECE_TITLES, half], F32, name="fold" + str(c) + "_" + str(half))
                 nc.gpsimd.tensor_tensor(shorter[:], folded[:, :, 0:half], folded[:, :, half : 2 * half], ALU.add)
                 folded = shorter[:]
-            nc.gpsimd.tensor_tensor(
-                den[:, h * (TITLES // FOLDS) : (h + 1) * (TITLES // FOLDS)].unsqueeze(2),
-                folded[:, :, 0:1],
-                folded[:, :, 1:2],
-                ALU.add,
-            )
+            nc.gpsimd.tensor_tensor(den[:, titles[c]].unsqueeze(2), folded[:, :, 0:1], folded[:, :, 1:2], ALU.add)
+        nc.vector.reduce_sum(den[:, titles[PIECES - 1]], words(e[:, pieces[PIECES - 1]]), axis=X)
 
         ev = held.tile([P, N], F32, name="ev")
         num = held.tile([P, TITLES], F32, name="num")

@@ -16,7 +16,6 @@ PIECE = 512
 PIECES = N // PIECE
 PIECE_TITLES = PIECE // WORDS
 BANKS = 8
-TABLE_LOADS = 2
 
 FLOPS = 2 * P * P * N + 2 * P * N + 2 * P * N + 2 * P * P * P + 2 * P * P * TITLES
 
@@ -36,9 +35,7 @@ def tile_nrmsmodel_kernel(tc, table, w, a, clicked, w_u, b_u, offs, out):
         a_row = held.tile([1, P], BF16, name="a_row")
         nc.scalar.dma_start(a_row[:], a.rearrange("k o -> o k"))
         table_sb = held.tile([P, V], BF16, name="table_sb")
-        for i in range(TABLE_LOADS):
-            columns = slice(i * (V // TABLE_LOADS), (i + 1) * (V // TABLE_LOADS))
-            nc.sync.dma_start(table_sb[:, columns], table[:, columns])
+        nc.sync.dma_start(table_sb[:], table)
         w_sb = held.tile([P, P], BF16, name="w_sb")
         nc.sync.dma_start(w_sb[:], w)
         w_u_sb = held.tile([P, P], BF16, name="w_u_sb")

@@ -8,6 +8,7 @@ EXP = mybir.ActivationFunctionType.Exp
 X = mybir.AxisListType.X
 
 P = 128
+HALF = P // 2
 V = 4096
 N = 2048
 WORDS = 16
@@ -16,6 +17,7 @@ PIECE = 512
 PIECES = N // PIECE
 PIECE_TITLES = PIECE // WORDS
 BANKS = 8
+ROWS = PIECES - 1
 
 FLOPS = 2 * P * P * N + 2 * P * N + 2 * P * N + 2 * P * P * P + 2 * P * P * TITLES
 
@@ -28,6 +30,7 @@ def tile_nrmsmodel_kernel(tc, table, w, a, clicked, w_u, b_u, offs, out):
     nc = tc.nc
     with (
         tc.tile_pool(name="held", bufs=1) as held,
+        tc.tile_pool(name="turn", bufs=1) as turn,
         tc.psum_pool(name="psum", bufs=BANKS) as psum,
     ):
         offsets = held.tile([P, N // 16], U16, name="offsets")
@@ -50,54 +53,83 @@ def tile_nrmsmodel_kernel(tc, table, w, a, clicked, w_u, b_u, offs, out):
         ones_f = held.tile([1, P], F32, name="ones_f")
         nc.vector.memset(ones_f[:], 1.0)
 
+        pick = held.tile([P, 2, P], F32, name="pick")
+        nc.gpsimd.memset(pick[:], 0.0)
+        for h in range(2):
+            nc.gpsimd.memset(pick[h * HALF : h * HALF + 1, h, :], 1.0)
+
         a_ps = psum.tile([P, P], F32, name="a_ps", tag="bank")
         nc.tensor.matmul(a_ps[:], a_row[:], ones_bf[:], start=True, stop=True)
         a_all = held.tile([P, P], BF16, name="a_all")
         nc.vector.tensor_copy(a_all[:], a_ps[:])
+        a_half = held.tile([P, 2, P], BF16, name="a_half")
+        nc.vector.memset(a_half[:], 0.0)
+        for h in range(2):
+            nc.vector.tensor_copy(a_half[:, h, h * HALF : (h + 1) * HALF], a_ps[:, h * HALF : (h + 1) * HALF])
 
-        pieces = [slice(c * PIECE, (c + 1) * PIECE) for c in range(PIECES)]
-        titles = [slice(c * PIECE_TITLES, (c + 1) * PIECE_TITLES) for c in range(PIECES)]
+        run = [slice(r * PIECE, (r + 1) * PIECE) for r in range(PIECES)]
+        run_titles = [slice(r * PIECE_TITLES, (r + 1) * PIECE_TITLES) for r in range(PIECES)]
         looked_up = [
             table_sb[:].indirect(offsets[:, c * (PIECE // 16) : (c + 1) * (PIECE // 16)]) for c in range(PIECES)
         ]
-        s_ps = [psum.tile([P, PIECE], F32, name="s_ps" + str(c), tag="bank") for c in range(PIECES)]
+        s_ps = [psum.tile([P, PIECE], F32, name="s_ps" + str(r), tag="bank") for r in range(ROWS)]
         v_ps = [psum.tile([P, PIECE], F32, name="v_ps" + str(c), tag="bank") for c in range(PIECES)]
-        for c in range(PIECES):
-            nc.tensor.matmul(s_ps[c][:], a_all[:], looked_up[c], start=True, stop=True)
+        for h in range(2):
+            nc.tensor.matmul(s_ps[0][:], a_half[:, h, :], looked_up[h], start=(h == 0), stop=(h == 1))
+        for r in range(1, ROWS):
+            nc.tensor.matmul(s_ps[r][:], a_all[:], looked_up[r + 1], start=True, stop=True)
         for c in range(PIECES):
             nc.tensor.matmul(v_ps[c][:], w_sb[:], looked_up[c], start=True, stop=True)
 
-        top = held.tile([P, TITLES], F32, name="top")
-        shifted = held.tile([P, N], F32, name="shifted")
-        e = held.tile([P, N], F32, name="e")
-        for c in range(PIECES):
-            nc.vector.reduce_max(top[:, titles[c]], words(s_ps[c][:]), axis=X)
+        top = held.tile([P, ROWS * PIECE_TITLES], F32, name="top")
+        shifted = held.tile([P, ROWS * PIECE], F32, name="shifted")
+        e = held.tile([P, ROWS * PIECE], F32, name="e")
+        for r in range(ROWS):
+            nc.vector.reduce_max(top[:, run_titles[r]], words(s_ps[r][:]), axis=X)
             nc.vector.tensor_tensor(
-                words(shifted[:, pieces[c]]),
-                words(s_ps[c][:]),
-                top[:, titles[c]].unsqueeze(2).to_broadcast([P, PIECE_TITLES, WORDS]),
+                words(shifted[:, run[r]]),
+                words(s_ps[r][:]),
+                top[:, run_titles[r]].unsqueeze(2).to_broadcast([P, PIECE_TITLES, WORDS]),
                 ALU.subtract,
             )
-            nc.scalar.activation(e[:, pieces[c]], shifted[:, pieces[c]], EXP, scale=1.0 / math.sqrt(P))
+            nc.scalar.activation(e[:, run[r]], shifted[:, run[r]], EXP, scale=1.0 / math.sqrt(P))
 
-        den = held.tile([P, TITLES], F32, name="den")
-        for c in range(PIECES - 1):
-            folded = words(e[:, pieces[c]])
+        e_ps = [psum.tile([P, PIECE], F32, name="e_ps" + str(h), tag="bank") for h in range(2)]
+        v_sb = held.tile([P, 2 * PIECE], F32, name="v_sb")
+        for h in range(2):
+            nc.tensor.matmul(e_ps[h][:], pick[:, h, :], e[:, run[0]], start=True, stop=True)
+            nc.scalar.copy(v_sb[:, run[h]], v_ps[h][:])
+
+        den = held.tile([P, ROWS * PIECE_TITLES], F32, name="den")
+        for first_bank, banks in ((0, 1), (1, ROWS - 1)):
+            folded = words(e[:, first_bank * PIECE : (first_bank + banks) * PIECE])
             for half in (8, 4, 2):
-                shorter = held.tile([P, PIECE_TITLES, half], F32, name="fold" + str(c) + "_" + str(half))
+                shorter = held.tile([P, banks * PIECE_TITLES, half], F32, name="fold" + str(first_bank) + "_" + str(half))
                 nc.gpsimd.tensor_tensor(shorter[:], folded[:, :, 0:half], folded[:, :, half : 2 * half], ALU.add)
                 folded = shorter[:]
-            nc.gpsimd.tensor_tensor(den[:, titles[c]].unsqueeze(2), folded[:, :, 0:1], folded[:, :, 1:2], ALU.add)
-        nc.vector.reduce_sum(den[:, titles[PIECES - 1]], words(e[:, pieces[PIECES - 1]]), axis=X)
+            nc.gpsimd.tensor_tensor(
+                den[:, first_bank * PIECE_TITLES : (first_bank + banks) * PIECE_TITLES].unsqueeze(2),
+                folded[:, :, 0:1],
+                folded[:, :, 1:2],
+                ALU.add,
+            )
+        den_ps = psum.tile([P, 2 * PIECE_TITLES], F32, name="den_ps", tag="bank")
+        for h in range(2):
+            nc.tensor.matmul(den_ps[:, run_titles[h]], pick[:, h, :], den[:, run_titles[0]], start=True, stop=True)
 
-        ev = held.tile([P, N], F32, name="ev")
+        ev = turn.tile([P, N], F32, name="ev", tag="turn")
         num = held.tile([P, TITLES], F32, name="num")
-        for c in range(PIECES):
-            nc.vector.tensor_tensor(ev[:, pieces[c]], v_ps[c][:], e[:, pieces[c]], ALU.mult)
-            nc.vector.reduce_sum(num[:, titles[c]], words(ev[:, pieces[c]]), axis=X)
+        for c in (2, 3, 0, 1):
+            if c >= 2:
+                nc.vector.tensor_tensor(ev[:, run[c]], v_ps[c][:], e[:, run[c - 1]], ALU.mult)
+            else:
+                nc.vector.tensor_tensor(ev[:, run[c]], e_ps[c][:], v_sb[:, run[c]], ALU.mult)
+            nc.vector.reduce_sum(num[:, run_titles[c]], words(ev[:, run[c]]), axis=X)
 
-        rden = held.tile([P, TITLES], F32, name="rden")
-        nc.vector.reciprocal(rden[:], den[:])
+        first = 2 * PIECE_TITLES
+        rden = turn.tile([P, TITLES], F32, name="rden", tag="turn")
+        nc.vector.reciprocal(rden[:, 0:first], den_ps[:])
+        nc.vector.reciprocal(rden[:, first:], den[:, PIECE_TITLES:])
         news_bf = held.tile([P, TITLES], BF16, name="news_bf")
         nc.vector.tensor_tensor(news_bf[:], num[:], rden[:], ALU.mult)
 

@@ -30,7 +30,6 @@ def tile_nrmsmodel_kernel(tc, table, w, a, clicked, w_u, b_u, offs, out):
     nc = tc.nc
     with (
         tc.tile_pool(name="held", bufs=1) as held,
-        tc.tile_pool(name="turn", bufs=1) as turn,
         tc.psum_pool(name="psum", bufs=BANKS) as psum,
     ):
         offsets = held.tile([P, N // 16], U16, name="offsets")
@@ -117,7 +116,7 @@ def tile_nrmsmodel_kernel(tc, table, w, a, clicked, w_u, b_u, offs, out):
         for h in range(2):
             nc.tensor.matmul(den_ps[:, run_titles[h]], pick[:, h, :], den[:, run_titles[0]], start=True, stop=True)
 
-        ev = turn.tile([P, N], F32, name="ev", tag="turn")
+        ev = held.tile([P, N], F32, name="ev")
         num = held.tile([P, TITLES], F32, name="num")
         for c in (2, 3, 0, 1):
             if c >= 2:
@@ -127,7 +126,7 @@ def tile_nrmsmodel_kernel(tc, table, w, a, clicked, w_u, b_u, offs, out):
             nc.vector.reduce_sum(num[:, run_titles[c]], words(ev[:, run[c]]), axis=X)
 
         first = 2 * PIECE_TITLES
-        rden = turn.tile([P, TITLES], F32, name="rden", tag="turn")
+        rden = held.tile([P, TITLES], F32, name="rden")
         nc.vector.reciprocal(rden[:, 0:first], den_ps[:])
         nc.vector.reciprocal(rden[:, first:], den[:, PIECE_TITLES:])
         news_bf = held.tile([P, TITLES], BF16, name="news_bf")

@@ -30,6 +30,7 @@ def tile_nrmsmodel_kernel(tc, table, w, a, clicked, w_u, b_u, offs, out):
     nc = tc.nc
     with (
         tc.tile_pool(name="held", bufs=1) as held,
+        tc.tile_pool(name="turn", bufs=1) as turn,
         tc.psum_pool(name="psum", bufs=BANKS) as psum,
     ):
         offsets = held.tile([P, N // 16], U16, name="offsets")
@@ -81,7 +82,7 @@ def tile_nrmsmodel_kernel(tc, table, w, a, clicked, w_u, b_u, offs, out):
             nc.tensor.matmul(v_ps[c][:], w_sb[:], looked_up[c], start=True, stop=True)
 
         top = held.tile([P, ROWS * PIECE_TITLES], F32, name="top")
-        shifted = held.tile([P, ROWS * PIECE], F32, name="shifted")
+        shifted = turn.tile([P, ROWS * PIECE], F32, name="shifted", tag="turn")
         e = held.tile([P, ROWS * PIECE], F32, name="e")
         for r in range(ROWS):
             nc.vector.reduce_max(top[:, run_titles[r]], words(s_ps[r][:]), axis=X)
@@ -94,7 +95,7 @@ def tile_nrmsmodel_kernel(tc, table, w, a, clicked, w_u, b_u, offs, out):
             nc.scalar.activation(e[:, run[r]], shifted[:, run[r]], EXP, scale=1.0 / math.sqrt(P))
 
         e_ps = [psum.tile([P, PIECE], F32, name="e_ps" + str(h), tag="bank") for h in range(2)]
-        v_sb = held.tile([P, 2 * PIECE], F32, name="v_sb")
+        v_sb = turn.tile([P, 2 * PIECE], F32, name="v_sb", tag="turn")
         for h in range(2):
             nc.tensor.matmul(e_ps[h][:], pick[:, h, :], e[:, run[0]], start=True, stop=True)
             nc.scalar.copy(v_sb[:, run[h]], v_ps[h][:])

@@ -9,6 +9,7 @@ X = mybir.AxisListType.X
 
 P = 128
 HALF = P // 2
+QUAD = P // 4
 V = 4096
 N = 2048
 WORDS = 16
@@ -17,7 +18,9 @@ PIECE = 512
 PIECES = N // PIECE
 PIECE_TITLES = PIECE // WORDS
 BANKS = 8
-ROWS = PIECES - 1
+
+FIRST, SHARED, LAST = 0, (1, 2), 3
+ROWS = {1: slice(HALF, HALF + QUAD), 2: slice(HALF + QUAD, P)}
 
 FLOPS = 2 * P * P * N + 2 * P * N + 2 * P * N + 2 * P * P * P + 2 * P * P * TITLES
 
@@ -53,91 +56,100 @@ def tile_nrmsmodel_kernel(tc, table, w, a, clicked, w_u, b_u, offs, out):
         ones_f = held.tile([1, P], F32, name="ones_f")
         nc.vector.memset(ones_f[:], 1.0)
 
-        pick = held.tile([P, 2, P], F32, name="pick")
-        nc.gpsimd.memset(pick[:], 0.0)
-        for h in range(2):
-            nc.gpsimd.memset(pick[h * HALF : h * HALF + 1, h, :], 1.0)
+        pick = {}
+        for c, row in ((FIRST, 0), (SHARED[0], HALF), (SHARED[1], HALF + QUAD)):
+            pick[c] = held.tile([P, P], F32, name="pick" + str(c))
+            nc.gpsimd.memset(pick[c][:], 0.0)
+            nc.gpsimd.memset(pick[c][row : row + 1, :], 1.0)
 
         a_ps = psum.tile([P, P], F32, name="a_ps", tag="bank")
         nc.tensor.matmul(a_ps[:], a_row[:], ones_bf[:], start=True, stop=True)
         a_all = held.tile([P, P], BF16, name="a_all")
         nc.vector.tensor_copy(a_all[:], a_ps[:])
-        a_half = held.tile([P, 2, P], BF16, name="a_half")
-        nc.vector.memset(a_half[:], 0.0)
-        for h in range(2):
-            nc.vector.tensor_copy(a_half[:, h, h * HALF : (h + 1) * HALF], a_ps[:, h * HALF : (h + 1) * HALF])
+        a_part = {}
+        for c in SHARED:
+            a_part[c] = held.tile([P, P], BF16, name="a_part" + str(c))
+            nc.vector.memset(a_part[c][:], 0.0)
+            nc.vector.tensor_copy(a_part[c][:, ROWS[c]], a_ps[:, ROWS[c]])
 
-        run = [slice(r * PIECE, (r + 1) * PIECE) for r in range(PIECES)]
-        run_titles = [slice(r * PIECE_TITLES, (r + 1) * PIECE_TITLES) for r in range(PIECES)]
+        run = [slice(c * PIECE, (c + 1) * PIECE) for c in range(PIECES)]
+        run_titles = [slice(c * PIECE_TITLES, (c + 1) * PIECE_TITLES) for c in range(PIECES)]
         looked_up = [
             table_sb[:].indirect(offsets[:, c * (PIECE // 16) : (c + 1) * (PIECE // 16)]) for c in range(PIECES)
         ]
-        s_ps = [psum.tile([P, PIECE], F32, name="s_ps" + str(r), tag="bank") for r in range(ROWS)]
+        s_first = psum.tile([P, PIECE], F32, name="s_first", tag="bank")
+        s_shared = psum.tile([P, PIECE], F32, name="s_shared", tag="bank")
+        s_last = psum.tile([P, PIECE], F32, name="s_last", tag="bank")
         v_ps = [psum.tile([P, PIECE], F32, name="v_ps" + str(c), tag="bank") for c in range(PIECES)]
-        for h in range(2):
-            nc.tensor.matmul(s_ps[0][:], a_half[:, h, :], looked_up[h], start=(h == 0), stop=(h == 1))
-        for r in range(1, ROWS):
-            nc.tensor.matmul(s_ps[r][:], a_all[:], looked_up[r + 1], start=True, stop=True)
+        nc.tensor.matmul(s_first[:], a_all[:], looked_up[FIRST], start=True, stop=True)
+        for c in SHARED:
+            nc.tensor.matmul(s_shared[:], a_part[c][:], looked_up[c], start=(c == SHARED[0]), stop=(c == SHARED[-1]))
+        nc.tensor.matmul(s_last[:], a_all[:], looked_up[LAST], start=True, stop=True)
         for c in range(PIECES):
             nc.tensor.matmul(v_ps[c][:], w_sb[:], looked_up[c], start=True, stop=True)
 
-        top = held.tile([P, ROWS * PIECE_TITLES], F32, name="top")
-        shifted = turn.tile([P, ROWS * PIECE], F32, name="shifted", tag="turn")
-        e = held.tile([P, ROWS * PIECE], F32, name="e")
-        for r in range(ROWS):
-            nc.vector.reduce_max(top[:, run_titles[r]], words(s_ps[r][:]), axis=X)
+        top_first = turn.tile([P, 2 * PIECE_TITLES], F32, name="top_first", tag="top")
+        top_later = turn.tile([P, 2 * PIECE_TITLES], F32, name="top_later", tag="top")
+        e_first = held.tile([P, PIECE], F32, name="e_first")
+        e_shared = held.tile([P, PIECE], F32, name="e_shared")
+        e_last = held.tile([P, PIECE], F32, name="e_last")
+        for bank, top, e, tag in (
+            (s_first, top_first[:, 0:PIECE_TITLES], e_first, "turn_first"),
+            (s_shared, top_later[:, 0:PIECE_TITLES], e_shared, "turn_shared"),
+            (s_last, top_later[:, PIECE_TITLES : 2 * PIECE_TITLES], e_last, "turn_last"),
+        ):
+            nc.vector.reduce_max(top, words(bank[:]), axis=X)
+            shifted = turn.tile([P, PIECE], F32, name="shifted", tag=tag)
             nc.vector.tensor_tensor(
-                words(shifted[:, run[r]]),
-                words(s_ps[r][:]),
-                top[:, run_titles[r]].unsqueeze(2).to_broadcast([P, PIECE_TITLES, WORDS]),
-                ALU.subtract,
+                words(shifted[:]), words(bank[:]), top.unsqueeze(2).to_broadcast([P, PIECE_TITLES, WORDS]), ALU.subtract
             )
-            nc.scalar.activation(e[:, run[r]], shifted[:, run[r]], EXP, scale=1.0 / math.sqrt(P))
+            nc.scalar.activation(e[:], shifted[:], EXP, scale=1.0 / math.sqrt(P))
 
-        e_ps = [psum.tile([P, PIECE], F32, name="e_ps" + str(h), tag="bank") for h in range(2)]
-        v_sb = turn.tile([P, 2 * PIECE], F32, name="v_sb", tag="turn")
-        for h in range(2):
-            nc.tensor.matmul(e_ps[h][:], pick[:, h, :], e[:, run[0]], start=True, stop=True)
-            nc.scalar.copy(v_sb[:, run[h]], v_ps[h][:])
-
-        den = held.tile([P, ROWS * PIECE_TITLES], F32, name="den")
-        for first_bank, banks in ((0, 1), (1, ROWS - 1)):
-            folded = words(e[:, first_bank * PIECE : (first_bank + banks) * PIECE])
-            for half in (8, 4, 2):
-                shorter = held.tile([P, banks * PIECE_TITLES, half], F32, name="fold" + str(first_bank) + "_" + str(half))
-                nc.gpsimd.tensor_tensor(shorter[:], folded[:, :, 0:half], folded[:, :, half : 2 * half], ALU.add)
-                folded = shorter[:]
-            nc.gpsimd.tensor_tensor(
-                den[:, first_bank * PIECE_TITLES : (first_bank + banks) * PIECE_TITLES].unsqueeze(2),
-                folded[:, :, 0:1],
-                folded[:, :, 1:2],
-                ALU.add,
-            )
-        den_ps = psum.tile([P, 2 * PIECE_TITLES], F32, name="den_ps", tag="bank")
-        for h in range(2):
-            nc.tensor.matmul(den_ps[:, run_titles[h]], pick[:, h, :], den[:, run_titles[0]], start=True, stop=True)
-
-        ev = held.tile([P, N], F32, name="ev")
-        num = held.tile([P, TITLES], F32, name="num")
-        for c in (2, 3, 0, 1):
-            if c >= 2:
-                nc.vector.tensor_tensor(ev[:, run[c]], v_ps[c][:], e[:, run[c - 1]], ALU.mult)
-            else:
-                nc.vector.tensor_tensor(ev[:, run[c]], e_ps[c][:], v_sb[:, run[c]], ALU.mult)
-            nc.vector.reduce_sum(num[:, run_titles[c]], words(ev[:, run[c]]), axis=X)
-
-        first = 2 * PIECE_TITLES
-        rden = held.tile([P, TITLES], F32, name="rden")
-        nc.vector.reciprocal(rden[:, 0:first], den_ps[:])
-        nc.vector.reciprocal(rden[:, first:], den[:, PIECE_TITLES:])
-        news_bf = held.tile([P, TITLES], BF16, name="news_bf")
-        nc.vector.tensor_tensor(news_bf[:], num[:], rden[:], ALU.mult)
+        e_ps, v_sb = {}, {}
+        for c, tag in ((SHARED[0], "turn_last"), (SHARED[1], "turn_shared")):
+            e_ps[c] = psum.tile([P, PIECE], F32, name="e_ps" + str(c), tag="bank")
+            nc.tensor.matmul(e_ps[c][:], pick[c][:], e_shared[:], start=True, stop=True)
+            v_sb[c] = turn.tile([P, PIECE], F32, name="v_sb" + str(c), tag=tag)
+            nc.scalar.copy(v_sb[c][:], v_ps[c][:])
 
         user_ps = psum.tile([P, P], F32, name="user_ps", tag="bank")
         nc.tensor.matmul(user_ps[:], w_u_sb[:], clicked_sb[:], start=True, stop=False)
         nc.tensor.matmul(user_ps[:], b_row[:], ones_f[:], start=False, stop=True)
         user_bf = held.tile([P, P], BF16, name="user_bf")
-        nc.vector.tensor_copy(user_bf[:], user_ps[:])
+        nc.scalar.copy(user_bf[:], user_ps[:])
+
+        den_last = held.tile([P, PIECE_TITLES], F32, name="den_last")
+        nc.vector.reduce_sum(den_last[:], words(e_last[:]), axis=X)
+        rden_last = held.tile([P, PIECE_TITLES], F32, name="rden_last")
+        nc.vector.reciprocal(rden_last[:], den_last[:])
+        folded = held.tile([P, PIECE_TITLES, 8], F32, name="fold8")
+        for e, rows in ((e_first, slice(0, HALF)), (e_shared, slice(HALF, P))):
+            whole = words(e[rows, :])
+            nc.gpsimd.tensor_tensor(folded[rows, :, :], whole[:, :, 0:8], whole[:, :, 8:16], ALU.add)
+        for half in (4, 2, 1):
+            shorter = held.tile([P, PIECE_TITLES, half], F32, name="fold" + str(half))
+            nc.gpsimd.tensor_tensor(shorter[:], folded[:, :, 0:half], folded[:, :, half : 2 * half], ALU.add)
+            folded = shorter
+
+        ev = held.tile([P, N], F32, name="ev")
+        num = held.tile([P, TITLES], F32, name="num")
+        for c in (FIRST, LAST, *SHARED):
+            if c in SHARED:
+                nc.vector.tensor_tensor(ev[:, run[c]], e_ps[c][:], v_sb[c][:], ALU.mult)
+            else:
+                nc.vector.tensor_tensor(ev[:, run[c]], v_ps[c][:], (e_first if c == FIRST else e_last)[:], ALU.mult)
+            if c == SHARED[0]:
+                rden = turn.tile([P, PIECE_TITLES], F32, name="rden", tag="turn_last")
+                nc.vector.reciprocal(rden[:], folded[:, :, 0])
+            nc.vector.reduce_sum(num[:, run_titles[c]], words(ev[:, run[c]]), axis=X)
+
+        rden_ps = psum.tile([P, LAST * PIECE_TITLES], F32, name="rden_ps", tag="bank")
+        for c in (FIRST, *SHARED):
+            nc.tensor.matmul(rden_ps[:, run_titles[c]], pick[c][:], rden[:], start=True, stop=True)
+        news_bf = held.tile([P, TITLES], BF16, name="news_bf")
+        nc.vector.tensor_tensor(news_bf[:, run_titles[LAST]], num[:, run_titles[LAST]], rden_last[:], ALU.mult)
+        others = slice(0, LAST * PIECE_TITLES)
+        nc.vector.tensor_tensor(news_bf[:, others], num[:, others], rden_ps[:], ALU.mult)
 
         logit_ps = psum.tile([P, TITLES], F32, name="logit_ps", tag="bank")
         nc.tensor.matmul(logit_ps[:], user_bf[:], news_bf[:], start=True, stop=True)

@@ -20,7 +20,7 @@ PIECE_TITLES = PIECE // WORDS
 BANKS = 8
 
 FIRST, SHARED, LAST = 0, (1, 2), 3
-ROWS = {1: slice(HALF, HALF + QUAD), 2: slice(HALF + QUAD, P)}
+QUAD_START = {0: 0, 3: QUAD, 1: HALF, 2: HALF + QUAD}
 
 FLOPS = 2 * P * P * N + 2 * P * N + 2 * P * N + 2 * P * P * P + 2 * P * P * TITLES
 
@@ -57,7 +57,8 @@ def tile_nrmsmodel_kernel(tc, table, w, a, clicked, w_u, b_u, offs, out):
         nc.vector.memset(ones_f[:], 1.0)
 
         pick = {}
-        for c, row in ((FIRST, 0), (SHARED[0], HALF), (SHARED[1], HALF + QUAD)):
+        for c in (*SHARED, FIRST, LAST):
+            row = QUAD_START[c]
             pick[c] = held.tile([P, P], F32, name="pick" + str(c))
             nc.gpsimd.memset(pick[c][:], 0.0)
             nc.gpsimd.memset(pick[c][row : row + 1, :], 1.0)
@@ -70,7 +71,8 @@ def tile_nrmsmodel_kernel(tc, table, w, a, clicked, w_u, b_u, offs, out):
         for c in SHARED:
             a_part[c] = held.tile([P, P], BF16, name="a_part" + str(c))
             nc.vector.memset(a_part[c][:], 0.0)
-            nc.vector.tensor_copy(a_part[c][:, ROWS[c]], a_ps[:, ROWS[c]])
+            quadrant = slice(QUAD_START[c], QUAD_START[c] + QUAD)
+            nc.vector.tensor_copy(a_part[c][:, quadrant], a_ps[:, quadrant])
 
         run = [slice(c * PIECE, (c + 1) * PIECE) for c in range(PIECES)]
         run_titles = [slice(c * PIECE_TITLES, (c + 1) * PIECE_TITLES) for c in range(PIECES)]
@@ -92,7 +94,7 @@ def tile_nrmsmodel_kernel(tc, table, w, a, clicked, w_u, b_u, offs, out):
         top_later = turn.tile([P, 2 * PIECE_TITLES], F32, name="top_later", tag="top")
         e_first = held.tile([P, PIECE], F32, name="e_first")
         e_shared = held.tile([P, PIECE], F32, name="e_shared")
-        e_last = held.tile([P, PIECE], F32, name="e_last")
+        e_last = turn.tile([P, PIECE], F32, name="e_last", tag="e_last")
         for bank, top, e, tag in (
             (s_first, top_first[:, 0:PIECE_TITLES], e_first, "turn_first"),
             (s_shared, top_later[:, 0:PIECE_TITLES], e_shared, "turn_shared"),
@@ -118,38 +120,43 @@ def tile_nrmsmodel_kernel(tc, table, w, a, clicked, w_u, b_u, offs, out):
         user_bf = held.tile([P, P], BF16, name="user_bf")
         nc.scalar.copy(user_bf[:], user_ps[:])
 
-        den_last = held.tile([P, PIECE_TITLES], F32, name="den_last")
-        nc.vector.reduce_sum(den_last[:], words(e_last[:]), axis=X)
-        rden_last = held.tile([P, PIECE_TITLES], F32, name="rden_last")
-        nc.vector.reciprocal(rden_last[:], den_last[:])
-        folded = held.tile([P, PIECE_TITLES, 8], F32, name="fold8")
-        for e, rows in ((e_first, slice(0, HALF)), (e_shared, slice(HALF, P))):
+        halved_e = held.tile([P, PIECE_TITLES, 8], F32, name="halved_e")
+        for e, rows in (
+            (e_first, slice(QUAD_START[FIRST], QUAD_START[FIRST] + QUAD)),
+            (e_shared, slice(QUAD_START[SHARED[0]], P)),
+            (e_last, slice(QUAD_START[LAST], QUAD_START[LAST] + QUAD)),
+        ):
             whole = words(e[rows, :])
-            nc.gpsimd.tensor_tensor(folded[rows, :, :], whole[:, :, 0:8], whole[:, :, 8:16], ALU.add)
-        for half in (4, 2, 1):
-            shorter = held.tile([P, PIECE_TITLES, half], F32, name="fold" + str(half))
-            nc.gpsimd.tensor_tensor(shorter[:], folded[:, :, 0:half], folded[:, :, half : 2 * half], ALU.add)
-            folded = shorter
+            nc.gpsimd.tensor_tensor(halved_e[rows, :, :], whole[:, :, 0:8], whole[:, :, 8:16], ALU.add)
 
-        ev = held.tile([P, N], F32, name="ev")
-        num = held.tile([P, TITLES], F32, name="num")
+        ev = [held.tile([P, PIECE], F32, name="ev" + str(c)) for c in range(PIECES)]
+        num = held.tile([P, LAST * PIECE_TITLES], F32, name="num")
+        rden_ps = psum.tile([P, TITLES], F32, name="rden_ps", tag="bank")
         for c in (FIRST, LAST, *SHARED):
             if c in SHARED:
-                nc.vector.tensor_tensor(ev[:, run[c]], e_ps[c][:], v_sb[c][:], ALU.mult)
+                nc.vector.tensor_tensor(ev[c][:], e_ps[c][:], v_sb[c][:], ALU.mult)
             else:
-                nc.vector.tensor_tensor(ev[:, run[c]], v_ps[c][:], (e_first if c == FIRST else e_last)[:], ALU.mult)
+                nc.vector.tensor_tensor(ev[c][:], v_ps[c][:], (e_first if c == FIRST else e_last)[:], ALU.mult)
+            if c == LAST:
+                halved_ev = held.tile([P, PIECE_TITLES, 8], F32, name="halved_ev")
+                product = words(ev[c][:])
+                nc.gpsimd.tensor_tensor(halved_ev[:], product[:, :, 0:8], product[:, :, 8:16], ALU.add)
+                continue
             if c == SHARED[0]:
-                rden = turn.tile([P, PIECE_TITLES], F32, name="rden", tag="turn_last")
-                nc.vector.reciprocal(rden[:], folded[:, :, 0])
-            nc.vector.reduce_sum(num[:, run_titles[c]], words(ev[:, run[c]]), axis=X)
+                den = turn.tile([P, PIECE_TITLES], F32, name="den", tag="e_last")
+                nc.vector.reduce_sum(den[:], halved_e[:], axis=X)
+                rden = held.tile([P, PIECE_TITLES], F32, name="rden")
+                nc.vector.reciprocal(rden[:], den[:])
+                for q in range(PIECES):
+                    nc.tensor.matmul(rden_ps[:, run_titles[q]], pick[q][:], rden[:], start=True, stop=True)
+            nc.vector.reduce_sum(num[:, run_titles[c]], words(ev[c][:]), axis=X)
+        num_last = turn.tile([P, PIECE_TITLES], F32, name="num_last", tag="turn_shared")
+        nc.vector.reduce_sum(num_last[:], halved_ev[:], axis=X)
 
-        rden_ps = psum.tile([P, LAST * PIECE_TITLES], F32, name="rden_ps", tag="bank")
-        for c in (FIRST, *SHARED):
-            nc.tensor.matmul(rden_ps[:, run_titles[c]], pick[c][:], rden[:], start=True, stop=True)
         news_bf = held.tile([P, TITLES], BF16, name="news_bf")
-        nc.vector.tensor_tensor(news_bf[:, run_titles[LAST]], num[:, run_titles[LAST]], rden_last[:], ALU.mult)
         others = slice(0, LAST * PIECE_TITLES)
-        nc.vector.tensor_tensor(news_bf[:, others], num[:, others], rden_ps[:], ALU.mult)
+        nc.vector.tensor_tensor(news_bf[:, run_titles[LAST]], num_last[:], rden_ps[:, run_titles[LAST]], ALU.mult)
+        nc.vector.tensor_tensor(news_bf[:, others], num[:], rden_ps[:, others], ALU.mult)
 
         logit_ps = psum.tile([P, TITLES], F32, name="logit_ps", tag="bank")
         nc.tensor.matmul(logit_ps[:], user_bf[:], news_bf[:], start=True, stop=True)

@@ -25,6 +25,14 @@ QUAD_START = {0: 0, 3: QUAD, 1: HALF, 2: HALF + QUAD}
 FLOPS = 2 * P * P * N + 2 * P * N + 2 * P * N + 2 * P * P * P + 2 * P * P * TITLES
 
 
+def list_columns(entries):
+    return slice(entries.start // 16, entries.stop // 16)
+
+
+def title_range(entries):
+    return slice(entries.start // WORDS, entries.stop // WORDS)
+
+
 def words(ap):
     return ap.rearrange("p (n t) -> p n t", t=WORDS)
 
@@ -75,15 +83,16 @@ def tile_nrmsmodel_kernel(tc, table, w, a, clicked, w_u, b_u, offs, out):
             nc.vector.tensor_copy(a_part[c][:, quadrant], a_ps[:, quadrant])
 
         run = [slice(c * PIECE, (c + 1) * PIECE) for c in range(PIECES)]
-        run_titles = [slice(c * PIECE_TITLES, (c + 1) * PIECE_TITLES) for c in range(PIECES)]
-        looked_up = [
-            table_sb[:].indirect(offsets[:, c * (PIECE // 16) : (c + 1) * (PIECE // 16)]) for c in range(PIECES)
-        ]
-        s_first = psum.tile([P, PIECE], F32, name="s_first", tag="bank")
+        run_titles = [title_range(r) for r in run]
+        looked_up = [table_sb[:].indirect(offsets[:, list_columns(r)]) for r in run]
+        parts = [slice(0, PIECE // 2), slice(PIECE // 2, PIECE)]
+        s_first = [psum.tile([P, PIECE // 2], F32, name="s_first" + str(h), tag="bank") for h in range(2)]
         s_shared = psum.tile([P, PIECE], F32, name="s_shared", tag="bank")
         s_last = psum.tile([P, PIECE], F32, name="s_last", tag="bank")
         v_ps = [psum.tile([P, PIECE], F32, name="v_ps" + str(c), tag="bank") for c in range(PIECES)]
-        nc.tensor.matmul(s_first[:], a_all[:], looked_up[FIRST], start=True, stop=True)
+        for h in range(2):
+            half_looked_up = table_sb[:].indirect(offsets[:, list_columns(parts[h])])
+            nc.tensor.matmul(s_first[h][:], a_all[:], half_looked_up, start=True, stop=True)
         for c in SHARED:
             nc.tensor.matmul(s_shared[:], a_part[c][:], looked_up[c], start=(c == SHARED[0]), stop=(c == SHARED[-1]))
         nc.tensor.matmul(s_last[:], a_all[:], looked_up[LAST], start=True, stop=True)
@@ -95,16 +104,20 @@ def tile_nrmsmodel_kernel(tc, table, w, a, clicked, w_u, b_u, offs, out):
         e_first = held.tile([P, PIECE], F32, name="e_first")
         e_shared = held.tile([P, PIECE], F32, name="e_shared")
         e_last = turn.tile([P, PIECE], F32, name="e_last", tag="e_last")
-        for bank, top, e, tag in (
-            (s_first, top_first[:, 0:PIECE_TITLES], e_first, "turn_first"),
-            (s_shared, top_later[:, 0:PIECE_TITLES], e_shared, "turn_shared"),
-            (s_last, top_later[:, PIECE_TITLES : 2 * PIECE_TITLES], e_last, "turn_last"),
+        whole = [run[0]]
+        for banks, entries, top, e, tag in (
+            (s_first, parts, top_first[:, 0:PIECE_TITLES], e_first, "turn_first"),
+            ([s_shared], whole, top_later[:, 0:PIECE_TITLES], e_shared, "turn_shared"),
+            ([s_last], whole, top_later[:, PIECE_TITLES : 2 * PIECE_TITLES], e_last, "turn_last"),
         ):
-            nc.vector.reduce_max(top, words(bank[:]), axis=X)
             shifted = turn.tile([P, PIECE], F32, name="shifted", tag=tag)
-            nc.vector.tensor_tensor(
-                words(shifted[:]), words(bank[:]), top.unsqueeze(2).to_broadcast([P, PIECE_TITLES, WORDS]), ALU.subtract
-            )
+            for bank, part in zip(banks, entries):
+                scores = words(bank[:])
+                tops = top[:, title_range(part)]
+                nc.vector.reduce_max(tops, scores, axis=X)
+                nc.vector.tensor_tensor(
+                    words(shifted[:, part]), scores, tops.unsqueeze(2).to_broadcast(list(scores.shape)), ALU.subtract
+                )
             nc.scalar.activation(e[:], shifted[:], EXP, scale=1.0 / math.sqrt(P))
 
         e_ps, v_sb = {}, {}
@@ -126,8 +139,8 @@ def tile_nrmsmodel_kernel(tc, table, w, a, clicked, w_u, b_u, offs, out):
             (e_shared, slice(QUAD_START[SHARED[0]], P)),
             (e_last, slice(QUAD_START[LAST], QUAD_START[LAST] + QUAD)),
         ):
-            whole = words(e[rows, :])
-            nc.gpsimd.tensor_tensor(halved_e[rows, :, :], whole[:, :, 0:8], whole[:, :, 8:16], ALU.add)
+            summands = words(e[rows, :])
+            nc.gpsimd.tensor_tensor(halved_e[rows, :, :], summands[:, :, 0:8], summands[:, :, 8:16], ALU.add)
 
         ev = [held.tile([P, PIECE], F32, name="ev" + str(c)) for c in range(PIECES)]
         num = held.tile([P, LAST * PIECE_TITLES], F32, name="num")
@@ -155,8 +168,8 @@ def tile_nrmsmodel_kernel(tc, table, w, a, clicked, w_u, b_u, offs, out):
 
         news_bf = held.tile([P, TITLES], BF16, name="news_bf")
         others = slice(0, LAST * PIECE_TITLES)
-        nc.vector.tensor_tensor(news_bf[:, run_titles[LAST]], num_last[:], rden_ps[:, run_titles[LAST]], ALU.mult)
         nc.vector.tensor_tensor(news_bf[:, others], num[:], rden_ps[:, others], ALU.mult)
+        nc.vector.tensor_tensor(news_bf[:, run_titles[LAST]], num_last[:], rden_ps[:, run_titles[LAST]], ALU.mult)
 
         logit_ps = psum.tile([P, TITLES], F32, name="logit_ps", tag="bank")
         nc.tensor.matmul(logit_ps[:], user_bf[:], news_bf[:], start=True, stop=True)

@@ -145,11 +145,15 @@ def tile_nrmsmodel_kernel(tc, table, w, a, clicked, w_u, b_u, offs, out):
         ev = [held.tile([P, PIECE], F32, name="ev" + str(c)) for c in range(PIECES)]
         num = held.tile([P, LAST * PIECE_TITLES], F32, name="num")
         rden_ps = psum.tile([P, TITLES], F32, name="rden_ps", tag="bank")
-        for c in (FIRST, LAST, *SHARED):
+        for part in parts:
+            nc.vector.tensor_tensor(ev[FIRST][:, part], v_ps[FIRST][:, part], e_first[:, part], ALU.mult)
+        for part in parts:
+            nc.vector.reduce_sum(num[:, title_range(part)], words(ev[FIRST][:, part]), axis=X)
+        for c in (LAST, *SHARED):
             if c in SHARED:
                 nc.vector.tensor_tensor(ev[c][:], e_ps[c][:], v_sb[c][:], ALU.mult)
             else:
-                nc.vector.tensor_tensor(ev[c][:], v_ps[c][:], (e_first if c == FIRST else e_last)[:], ALU.mult)
+                nc.vector.tensor_tensor(ev[c][:], v_ps[c][:], e_last[:], ALU.mult)
             if c == LAST:
                 halved_ev = held.tile([P, PIECE_TITLES, 8], F32, name="halved_ev")
                 product = words(ev[c][:])

@@ -88,36 +88,41 @@ def tile_nrmsmodel_kernel(tc, table, w, a, clicked, w_u, b_u, offs, out):
         parts = [slice(0, PIECE // 2), slice(PIECE // 2, PIECE)]
         s_first = [psum.tile([P, PIECE // 2], F32, name="s_first" + str(h), tag="bank") for h in range(2)]
         s_shared = psum.tile([P, PIECE], F32, name="s_shared", tag="bank")
-        s_last = psum.tile([P, PIECE], F32, name="s_last", tag="bank")
+        s_last = [psum.tile([P, PIECE // 2], F32, name="s_last" + str(h), tag="bank") for h in range(2)]
         v_ps = [psum.tile([P, PIECE], F32, name="v_ps" + str(c), tag="bank") for c in range(PIECES)]
-        for h in range(2):
-            half_looked_up = table_sb[:].indirect(offsets[:, list_columns(parts[h])])
-            nc.tensor.matmul(s_first[h][:], a_all[:], half_looked_up, start=True, stop=True)
+        def scores_of_part(bank, c, part):
+            entries = slice(run[c].start + part.start, run[c].start + part.stop)
+            looked_up_part = table_sb[:].indirect(offsets[:, list_columns(entries)])
+            nc.tensor.matmul(bank[:], a_all[:], looked_up_part, start=True, stop=True)
+
+        scores_of_part(s_first[0], FIRST, parts[0])
+        scores_of_part(s_first[1], FIRST, parts[1])
+        scores_of_part(s_last[0], LAST, parts[0])
         for c in SHARED:
             nc.tensor.matmul(s_shared[:], a_part[c][:], looked_up[c], start=(c == SHARED[0]), stop=(c == SHARED[-1]))
-        nc.tensor.matmul(s_last[:], a_all[:], looked_up[LAST], start=True, stop=True)
+        scores_of_part(s_last[1], LAST, parts[1])
         for c in range(PIECES):
             nc.tensor.matmul(v_ps[c][:], w_sb[:], looked_up[c], start=True, stop=True)
 
-        top_first = turn.tile([P, 2 * PIECE_TITLES], F32, name="top_first", tag="top")
-        top_later = turn.tile([P, 2 * PIECE_TITLES], F32, name="top_later", tag="top")
+        top = held.tile([P, 3 * PIECE_TITLES], F32, name="top")
+        shifted_first = turn.tile([P, PIECE], F32, name="shifted_first", tag="turn_first")
+        shifted_shared = turn.tile([P, PIECE], F32, name="shifted_shared", tag="turn_shared")
+        shifted_last = turn.tile([P, PIECE], F32, name="shifted_last", tag="turn_last")
         e_first = held.tile([P, PIECE], F32, name="e_first")
         e_shared = held.tile([P, PIECE], F32, name="e_shared")
         e_last = turn.tile([P, PIECE], F32, name="e_last", tag="e_last")
-        whole = [run[0]]
-        for banks, entries, top, e, tag in (
-            (s_first, parts, top_first[:, 0:PIECE_TITLES], e_first, "turn_first"),
-            ([s_shared], whole, top_later[:, 0:PIECE_TITLES], e_shared, "turn_shared"),
-            ([s_last], whole, top_later[:, PIECE_TITLES : 2 * PIECE_TITLES], e_last, "turn_last"),
+        half = PIECE_TITLES // 2
+        for bank, tops, shifted in (
+            (s_first[0], top[:, 0:half], shifted_first[:, parts[0]]),
+            (s_first[1], top[:, half : 2 * half], shifted_first[:, parts[1]]),
+            (s_last[0], top[:, 2 * half : 3 * half], shifted_last[:, parts[0]]),
+            (s_shared, top[:, 3 * half : 5 * half], shifted_shared[:]),
+            (s_last[1], top[:, 5 * half : 6 * half], shifted_last[:, parts[1]]),
         ):
-            shifted = turn.tile([P, PIECE], F32, name="shifted", tag=tag)
-            for bank, part in zip(banks, entries):
-                scores = words(bank[:])
-                tops = top[:, title_range(part)]
-                nc.vector.reduce_max(tops, scores, axis=X)
-                nc.vector.tensor_tensor(
-                    words(shifted[:, part]), scores, tops.unsqueeze(2).to_broadcast(list(scores.shape)), ALU.subtract
-                )
+            scores = words(bank[:])
+            nc.vector.reduce_max(tops, scores, axis=X)
+            nc.vector.tensor_tensor(words(shifted), scores, tops.unsqueeze(2).to_broadcast(list(scores.shape)), ALU.subtract)
+        for e, shifted in ((e_first, shifted_first), (e_shared, shifted_shared), (e_last, shifted_last)):
             nc.scalar.activation(e[:], shifted[:], EXP, scale=1.0 / math.sqrt(P))
 
         e_ps, v_sb = {}, {}

@@ -95,12 +95,12 @@ def tile_nrmsmodel_kernel(tc, table, w, a, clicked, w_u, b_u, offs, out):
             looked_up_part = table_sb[:].indirect(offsets[:, list_columns(entries)])
             nc.tensor.matmul(bank[:], a_all[:], looked_up_part, start=True, stop=True)
 
-        scores_of_part(s_first[0], FIRST, parts[0])
-        scores_of_part(s_first[1], FIRST, parts[1])
-        scores_of_part(s_last[0], LAST, parts[0])
+        for h in range(2):
+            scores_of_part(s_first[h], FIRST, parts[h])
         for c in SHARED:
             nc.tensor.matmul(s_shared[:], a_part[c][:], looked_up[c], start=(c == SHARED[0]), stop=(c == SHARED[-1]))
-        scores_of_part(s_last[1], LAST, parts[1])
+        for h in range(2):
+            scores_of_part(s_last[h], LAST, parts[h])
         for c in range(PIECES):
             nc.tensor.matmul(v_ps[c][:], w_sb[:], looked_up[c], start=True, stop=True)
 
@@ -115,8 +115,8 @@ def tile_nrmsmodel_kernel(tc, table, w, a, clicked, w_u, b_u, offs, out):
         for bank, tops, shifted in (
             (s_first[0], top[:, 0:half], shifted_first[:, parts[0]]),
             (s_first[1], top[:, half : 2 * half], shifted_first[:, parts[1]]),
-            (s_last[0], top[:, 2 * half : 3 * half], shifted_last[:, parts[0]]),
-            (s_shared, top[:, 3 * half : 5 * half], shifted_shared[:]),
+            (s_shared, top[:, 2 * half : 4 * half], shifted_shared[:]),
+            (s_last[0], top[:, 4 * half : 5 * half], shifted_last[:, parts[0]]),
             (s_last[1], top[:, 5 * half : 6 * half], shifted_last[:, parts[1]]),
         ):
             scores = words(bank[:])
@@ -126,7 +126,7 @@ def tile_nrmsmodel_kernel(tc, table, w, a, clicked, w_u, b_u, offs, out):
             nc.scalar.activation(e[:], shifted[:], EXP, scale=1.0 / math.sqrt(P))
 
         e_ps, v_sb = {}, {}
-        for c, tag in ((SHARED[0], "turn_last"), (SHARED[1], "turn_shared")):
+        for c, tag in ((SHARED[0], "turn_shared"), (SHARED[1], "turn_last")):
             e_ps[c] = psum.tile([P, PIECE], F32, name="e_ps" + str(c), tag="bank")
             nc.tensor.matmul(e_ps[c][:], pick[c][:], e_shared[:], start=True, stop=True)
             v_sb[c] = turn.tile([P, PIECE], F32, name="v_sb" + str(c), tag=tag)
@@ -148,37 +148,40 @@ def tile_nrmsmodel_kernel(tc, table, w, a, clicked, w_u, b_u, offs, out):
             nc.gpsimd.tensor_tensor(halved_e[rows, :, :], summands[:, :, 0:8], summands[:, :, 8:16], ALU.add)
 
         ev = [held.tile([P, PIECE], F32, name="ev" + str(c)) for c in range(PIECES)]
-        num = held.tile([P, LAST * PIECE_TITLES], F32, name="num")
-        rden_ps = psum.tile([P, TITLES], F32, name="rden_ps", tag="bank")
+        halved_ev = [held.tile([P, PIECE_TITLES, 8], F32, name="halved_ev" + str(c)) for c in (1, 3)]
+        num_even = held.tile([P, 2, PIECE_TITLES], F32, name="num_even")
+
+        def halve(c):
+            product = words(ev[c][:])
+            nc.gpsimd.tensor_tensor(halved_ev[c // 2][:], product[:, :, 0:8], product[:, :, 8:16], ALU.add)
+
         for part in parts:
             nc.vector.tensor_tensor(ev[FIRST][:, part], v_ps[FIRST][:, part], e_first[:, part], ALU.mult)
         for part in parts:
-            nc.vector.reduce_sum(num[:, title_range(part)], words(ev[FIRST][:, part]), axis=X)
-        for c in (LAST, *SHARED):
-            if c in SHARED:
-                nc.vector.tensor_tensor(ev[c][:], e_ps[c][:], v_sb[c][:], ALU.mult)
-            else:
-                nc.vector.tensor_tensor(ev[c][:], v_ps[c][:], e_last[:], ALU.mult)
-            if c == LAST:
-                halved_ev = held.tile([P, PIECE_TITLES, 8], F32, name="halved_ev")
-                product = words(ev[c][:])
-                nc.gpsimd.tensor_tensor(halved_ev[:], product[:, :, 0:8], product[:, :, 8:16], ALU.add)
-                continue
-            if c == SHARED[0]:
-                den = turn.tile([P, PIECE_TITLES], F32, name="den", tag="e_last")
-                nc.vector.reduce_sum(den[:], halved_e[:], axis=X)
-                rden = held.tile([P, PIECE_TITLES], F32, name="rden")
-                nc.vector.reciprocal(rden[:], den[:])
-                for q in range(PIECES):
-                    nc.tensor.matmul(rden_ps[:, run_titles[q]], pick[q][:], rden[:], start=True, stop=True)
-            nc.vector.reduce_sum(num[:, run_titles[c]], words(ev[c][:]), axis=X)
-        num_last = turn.tile([P, PIECE_TITLES], F32, name="num_last", tag="turn_shared")
-        nc.vector.reduce_sum(num_last[:], halved_ev[:], axis=X)
+            nc.vector.reduce_sum(num_even[:, 0, title_range(part)], words(ev[FIRST][:, part]), axis=X)
+        nc.vector.tensor_tensor(ev[LAST][:], v_ps[LAST][:], e_last[:], ALU.mult)
+        halve(LAST)
+        nc.vector.tensor_tensor(ev[1][:], e_ps[1][:], v_sb[1][:], ALU.mult)
+        halve(1)
+
+        den = turn.tile([P, PIECE_TITLES], F32, name="den", tag="e_last")
+        nc.vector.reduce_sum(den[:], halved_e[:], axis=X)
+        rden = held.tile([P, PIECE_TITLES], F32, name="rden")
+        nc.vector.reciprocal(rden[:], den[:])
+        rden_ps = psum.tile([P, 2, 2, PIECE_TITLES], F32, name="rden_ps", tag="bank")
+        for c in range(PIECES):
+            nc.tensor.matmul(rden_ps[:, c // 2, c % 2, :], pick[c][:], rden[:], start=True, stop=True)
+
+        nc.vector.tensor_tensor(ev[2][:], e_ps[2][:], v_sb[2][:], ALU.mult)
+        nc.vector.reduce_sum(num_even[:, 1, :], words(ev[2][:]), axis=X)
+        num_odd = turn.tile([P, 2, PIECE_TITLES], F32, name="num_odd", tag="turn_last")
+        for c in (LAST, 1):
+            nc.vector.reduce_sum(num_odd[:, c // 2, :], halved_ev[c // 2][:], axis=X)
 
         news_bf = held.tile([P, TITLES], BF16, name="news_bf")
-        others = slice(0, LAST * PIECE_TITLES)
-        nc.vector.tensor_tensor(news_bf[:, others], num[:], rden_ps[:, others], ALU.mult)
-        nc.vector.tensor_tensor(news_bf[:, run_titles[LAST]], num_last[:], rden_ps[:, run_titles[LAST]], ALU.mult)
+        news = news_bf[:].rearrange("p (i j n) -> p i j n", i=2, j=2)
+        nc.vector.tensor_tensor(news[:, :, 0, :], num_even[:], rden_ps[:, :, 0, :], ALU.mult)
+        nc.vector.tensor_tensor(news[:, :, 1, :], num_odd[:], rden_ps[:, :, 1, :], ALU.mult)
 
         logit_ps = psum.tile([P, TITLES], F32, name="logit_ps", tag="bank")
         nc.tensor.matmul(logit_ps[:], user_bf[:], news_bf[:], start=True, stop=True)

import math

import concourse.mybir as mybir

BF16, F32, U16 = mybir.dt.bfloat16, mybir.dt.float32, mybir.dt.uint16
ALU = mybir.AluOpType
EXP = mybir.ActivationFunctionType.Exp
X = mybir.AxisListType.X

P = 128
HALF = P // 2
QUAD = P // 4
V = 4096
N = 2048
WORDS = 16
TITLES = N // WORDS
PIECE = 512
PIECES = N // PIECE
PIECE_TITLES = PIECE // WORDS
BANKS = 8

FIRST, SHARED, LAST = 0, (1, 2), 3
QUAD_START = {0: 0, 3: QUAD, 1: HALF, 2: HALF + QUAD}

FLOPS = 2 * P * P * N + 2 * P * N + 2 * P * N + 2 * P * P * P + 2 * P * P * TITLES


def list_columns(entries):
    return slice(entries.start // 16, entries.stop // 16)


def title_range(entries):
    return slice(entries.start // WORDS, entries.stop // WORDS)


def words(ap):
    return ap.rearrange("p (n t) -> p n t", t=WORDS)


def tile_nrmsmodel_kernel(tc, table, w, a, clicked, w_u, b_u, offs, out):
    nc = tc.nc
    with (
        tc.tile_pool(name="held", bufs=1) as held,
        tc.tile_pool(name="turn", bufs=1) as turn,
        tc.psum_pool(name="psum", bufs=BANKS) as psum,
    ):
        offsets = held.tile([P, N // 16], U16, name="offsets")
        nc.sync.dma_start(offsets[:], offs)
        a_row = held.tile([1, P], BF16, name="a_row")
        nc.scalar.dma_start(a_row[:], a.rearrange("k o -> o k"))
        table_sb = held.tile([P, V], BF16, name="table_sb")
        nc.sync.dma_start(table_sb[:], table)
        w_sb = held.tile([P, P], BF16, name="w_sb")
        nc.sync.dma_start(w_sb[:], w)
        w_u_sb = held.tile([P, P], BF16, name="w_u_sb")
        nc.sync.dma_start(w_u_sb[:], w_u)
        clicked_sb = held.tile([P, P], BF16, name="clicked_sb")
        nc.sync.dma_start(clicked_sb[:], clicked)
        b_row = held.tile([1, P], F32, name="b_row")
        nc.sync.dma_start(b_row[:], b_u.rearrange("m o -> o m"))

        ones_bf = held.tile([1, P], BF16, name="ones_bf")
        nc.vector.memset(ones_bf[:], 1.0)
        ones_f = held.tile([1, P], F32, name="ones_f")
        nc.vector.memset(ones_f[:], 1.0)

        pick = {}
        for c in (*SHARED, FIRST, LAST):
            row = QUAD_START[c]
            pick[c] = held.tile([P, P], F32, name="pick" + str(c))
            nc.gpsimd.memset(pick[c][:], 0.0)
            nc.gpsimd.memset(pick[c][row : row + 1, :], 1.0)

        a_ps = psum.tile([P, P], F32, name="a_ps", tag="bank")
        nc.tensor.matmul(a_ps[:], a_row[:], ones_bf[:], start=True, stop=True)
        a_all = held.tile([P, P], BF16, name="a_all")
        nc.vector.tensor_copy(a_all[:], a_ps[:])
        a_part = {}
        for c in SHARED:
            a_part[c] = held.tile([P, P], BF16, name="a_part" + str(c))
            nc.vector.memset(a_part[c][:], 0.0)
            quadrant = slice(QUAD_START[c], QUAD_START[c] + QUAD)
            nc.vector.tensor_copy(a_part[c][:, quadrant], a_ps[:, quadrant])

        run = [slice(c * PIECE, (c + 1) * PIECE) for c in range(PIECES)]
        run_titles = [title_range(r) for r in run]
        looked_up = [table_sb[:].indirect(offsets[:, list_columns(r)]) for r in run]
        parts = [slice(0, PIECE // 2), slice(PIECE // 2, PIECE)]
        s_first = [psum.tile([P, PIECE // 2], F32, name="s_first" + str(h), tag="bank") for h in range(2)]
        s_shared = psum.tile([P, PIECE], F32, name="s_shared", tag="bank")
        s_last = [psum.tile([P, PIECE // 2], F32, name="s_last" + str(h), tag="bank") for h in range(2)]
        v_ps = [psum.tile([P, PIECE], F32, name="v_ps" + str(c), tag="bank") for c in range(PIECES)]
        def scores_of_part(bank, c, part):
            entries = slice(run[c].start + part.start, run[c].start + part.stop)
            looked_up_part = table_sb[:].indirect(offsets[:, list_columns(entries)])
            nc.tensor.matmul(bank[:], a_all[:], looked_up_part, start=True, stop=True)

        for h in range(2):
            scores_of_part(s_first[h], FIRST, parts[h])
        for c in SHARED:
            nc.tensor.matmul(s_shared[:], a_part[c][:], looked_up[c], start=(c == SHARED[0]), stop=(c == SHARED[-1]))
        for h in range(2):
            scores_of_part(s_last[h], LAST, parts[h])
        for c in range(PIECES):
            nc.tensor.matmul(v_ps[c][:], w_sb[:], looked_up[c], start=True, stop=True)

        top = held.tile([P, 3 * PIECE_TITLES], F32, name="top")
        shifted_first = turn.tile([P, PIECE], F32, name="shifted_first", tag="turn_first")
        shifted_shared = turn.tile([P, PIECE], F32, name="shifted_shared", tag="turn_shared")
        shifted_last = turn.tile([P, PIECE], F32, name="shifted_last", tag="turn_last")
        e_first = held.tile([P, PIECE], F32, name="e_first")
        e_shared = held.tile([P, PIECE], F32, name="e_shared")
        e_last = turn.tile([P, PIECE], F32, name="e_last", tag="e_last")
        half = PIECE_TITLES // 2
        for bank, tops, shifted in (
            (s_first[0], top[:, 0:half], shifted_first[:, parts[0]]),
            (s_first[1], top[:, half : 2 * half], shifted_first[:, parts[1]]),
            (s_shared, top[:, 2 * half : 4 * half], shifted_shared[:]),
            (s_last[0], top[:, 4 * half : 5 * half], shifted_last[:, parts[0]]),
            (s_last[1], top[:, 5 * half : 6 * half], shifted_last[:, parts[1]]),
        ):
            scores = words(bank[:])
            nc.vector.reduce_max(tops, scores, axis=X)
            nc.vector.tensor_tensor(words(shifted), scores, tops.unsqueeze(2).to_broadcast(list(scores.shape)), ALU.subtract)
        for e, shifted in ((e_first, shifted_first), (e_shared, shifted_shared), (e_last, shifted_last)):
            nc.scalar.activation(e[:], shifted[:], EXP, scale=1.0 / math.sqrt(P))

        e_ps, v_sb = {}, {}
        for c, tag in ((SHARED[0], "turn_shared"), (SHARED[1], "turn_last")):
            e_ps[c] = psum.tile([P, PIECE], F32, name="e_ps" + str(c), tag="bank")
            nc.tensor.matmul(e_ps[c][:], pick[c][:], e_shared[:], start=True, stop=True)
            v_sb[c] = turn.tile([P, PIECE], F32, name="v_sb" + str(c), tag=tag)
            nc.scalar.copy(v_sb[c][:], v_ps[c][:])

        user_ps = psum.tile([P, P], F32, name="user_ps", tag="bank")
        nc.tensor.matmul(user_ps[:], w_u_sb[:], clicked_sb[:], start=True, stop=False)
        nc.tensor.matmul(user_ps[:], b_row[:], ones_f[:], start=False, stop=True)
        user_bf = held.tile([P, P], BF16, name="user_bf")
        nc.scalar.copy(user_bf[:], user_ps[:])

        halved_e = held.tile([P, PIECE_TITLES, 8], F32, name="halved_e")
        for e, rows in (
            (e_first, slice(QUAD_START[FIRST], QUAD_START[FIRST] + QUAD)),
            (e_shared, slice(QUAD_START[SHARED[0]], P)),
            (e_last, slice(QUAD_START[LAST], QUAD_START[LAST] + QUAD)),
        ):
            summands = words(e[rows, :])
            nc.gpsimd.tensor_tensor(halved_e[rows, :, :], summands[:, :, 0:8], summands[:, :, 8:16], ALU.add)

        ev = [held.tile([P, PIECE], F32, name="ev" + str(c)) for c in range(PIECES)]
        halved_ev = [held.tile([P, PIECE_TITLES, 8], F32, name="halved_ev" + str(c)) for c in (1, 3)]
        num_even = held.tile([P, 2, PIECE_TITLES], F32, name="num_even")

        def halve(c):
            product = words(ev[c][:])
            nc.gpsimd.tensor_tensor(halved_ev[c // 2][:], product[:, :, 0:8], product[:, :, 8:16], ALU.add)

        for part in parts:
            nc.vector.tensor_tensor(ev[FIRST][:, part], v_ps[FIRST][:, part], e_first[:, part], ALU.mult)
        for part in parts:
            nc.vector.reduce_sum(num_even[:, 0, title_range(part)], words(ev[FIRST][:, part]), axis=X)
        nc.vector.tensor_tensor(ev[LAST][:], v_ps[LAST][:], e_last[:], ALU.mult)
        halve(LAST)
        nc.vector.tensor_tensor(ev[1][:], e_ps[1][:], v_sb[1][:], ALU.mult)
        halve(1)

        den = turn.tile([P, PIECE_TITLES], F32, name="den", tag="e_last")
        nc.vector.reduce_sum(den[:], halved_e[:], axis=X)
        rden = held.tile([P, PIECE_TITLES], F32, name="rden")
        nc.vector.reciprocal(rden[:], den[:])
        rden_ps = psum.tile([P, 2, 2, PIECE_TITLES], F32, name="rden_ps", tag="bank")
        for c in range(PIECES):
            nc.tensor.matmul(rden_ps[:, c // 2, c % 2, :], pick[c][:], rden[:], start=True, stop=True)

        nc.vector.tensor_tensor(ev[2][:], e_ps[2][:], v_sb[2][:], ALU.mult)
        nc.vector.reduce_sum(num_even[:, 1, :], words(ev[2][:]), axis=X)
        num_odd = turn.tile([P, 2, PIECE_TITLES], F32, name="num_odd", tag="turn_last")
        for c in (LAST, 1):
            nc.vector.reduce_sum(num_odd[:, c // 2, :], halved_ev[c // 2][:], axis=X)

        news_bf = held.tile([P, TITLES], BF16, name="news_bf")
        news = news_bf[:].rearrange("p (i j n) -> p i j n", i=2, j=2)
        nc.vector.tensor_tensor(news[:, :, 0, :], num_even[:], rden_ps[:, :, 0, :], ALU.mult)
        nc.vector.tensor_tensor(news[:, :, 1, :], num_odd[:], rden_ps[:, :, 1, :], ALU.mult)

        logit_ps = psum.tile([P, TITLES], F32, name="logit_ps", tag="bank")
        nc.tensor.matmul(logit_ps[:], user_bf[:], news_bf[:], start=True, stop=True)
        neg_max = held.tile([P, 1], F32, name="neg_max")
        nc.vector.reduce_max(neg_max[:], logit_ps[:], axis=X, negate=True)
        el = held.tile([P, TITLES], F32, name="el")
        el_sum = held.tile([P, 1], F32, name="el_sum")
        nc.scalar.activation(el[:], logit_ps[:], EXP, bias=neg_max[:], accum_out=el_sum[:])
        r_sum = held.tile([P, 1], F32, name="r_sum")
        nc.vector.reciprocal(r_sum[:], el_sum[:])
        out_sb = held.tile([P, TITLES], F32, name="out_sb")
        nc.vector.tensor_scalar_mul(out_sb[:], el[:], r_sum[:])
        nc.sync.dma_start(out, out_sb[:])
